import numpy as np
import ml_dtypes


def mxq(x, axis, fmt="e4m3"):
    dtype, down = {"e4m3": (ml_dtypes.float8_e4m3fn, 7), "e5m2": (ml_dtypes.float8_e5m2, 14)}[fmt]
    v = np.moveaxis(np.asarray(x, np.float32).astype(ml_dtypes.bfloat16).astype(np.float64), axis, -1)
    blocks = v.reshape(v.shape[:-1] + (-1, 32))
    amax = np.abs(blocks).max(-1, keepdims=True)
    byte = np.maximum(np.where(amax > 0, np.frexp(amax)[1] - 1 + 127, 0) - down, 1)
    scale = np.exp2(byte - 127.0)
    codes = (blocks / scale).astype(np.float32).astype(dtype).astype(np.float64)
    return np.moveaxis((codes * scale).reshape(v.shape), -1, axis)


WIDE = False


def mx_kscale(k):
    if not WIDE:
        return np.ones(k)
    levels = np.array([10, -10, 5, -5, 0])
    a = np.random.permutation(np.resize(levels, k // 512 * 4)).reshape(k // 512, 4)
    idx = np.arange(k)
    return np.exp2(a[idx // 512, idx % 128 // 32])


BF16 = ml_dtypes.bfloat16


def bf(x):
    return np.asarray(x, np.float32).astype(BF16)


def f64(x):
    return np.asarray(x).astype(np.float64)


B, IMG, P0, P1, C, F = 8, 512, 8, 16, 4, 512
E0, E1 = IMG // P0, IMG // P1
N0, N1 = E0 * E0, E1 * E1
D0, D1 = P0 * P0 * C, P1 * P1 * C


def setup_inputs():
    s = mx_kscale(D1)
    flat = np.random.standard_normal((B, N1, D1)) * s
    img = flat.reshape(B, E1, E1, P1, P1, C).transpose(0, 1, 3, 2, 4, 5).reshape(B, IMG, IMG, C)
    encoded = img.reshape(B, E0, P0, E0, P0, C).transpose(0, 1, 3, 2, 4, 5).reshape(B, N0, D0)
    return {"encoded": bf(encoded),
            "W": bf(np.random.standard_normal((D1, F)) / np.sqrt(D1) / s[:, None]),
            "b": bf(np.random.standard_normal(F) * 0.3),
            "pos_emb": bf(np.random.standard_normal((N1, F)) * 0.5)}


def reference(encoded, W, b, pos_emb):
    x = f64(encoded).reshape(-1, E0, E0, P0, P0, C)
    img = x.transpose(0, 1, 3, 2, 4, 5).reshape(-1, IMG, IMG, C)
    new_patches = img.reshape(-1, E1, P1, E1, P1, C).transpose(0, 1, 3, 2, 4, 5)
    flat = new_patches.reshape(-1, N1, D1)
    return (mxq(flat, 2, "e4m3") @ mxq(f64(W), 0, "e4m3")) + f64(b) + f64(pos_emb)

@@ -1,0 +1,235 @@
+from contextlib import ExitStack
+
+import concourse.mybir as mybir
+from concourse.masks import make_identity
+
+FLOPS = 2 * 8 * 1024 * 1024 * 512
+
+BF16 = mybir.dt.bfloat16
+F32 = mybir.dt.float32
+U32 = mybir.dt.uint32
+U8 = mybir.dt.uint8
+FP8X4 = mybir.dt.float8_e4m3fn_x4
+ADD = mybir.AluOpType.add
+
+P = 128
+IMAGES = 8
+TILES = 8
+GROUP = 4
+PER_IMAGE = TILES // GROUP
+GROUPS = IMAGES * PER_IMAGE
+FOUT = 512
+X_BUFS = 4
+O_BUFS = 6
+NSORT = 0
+FIRST_SORTED = 2
+
+
+def tile_resampling_t_kernel(tc, encoded, W, b, pos_emb, out):
+    nc = tc.nc
+    with ExitStack() as ctx:
+        const = ctx.enter_context(tc.tile_pool(name="const", bufs=1))
+        xpool = ctx.enter_context(tc.tile_pool(name="xpool", bufs=X_BUFS))
+        spool = ctx.enter_context(tc.tile_pool(name="spool", bufs=2 * NSORT)) if NSORT else None
+        gpool = ctx.enter_context(tc.tile_pool(name="gpool", bufs=3))
+        opool = ctx.enter_context(tc.tile_pool(name="opool", bufs=O_BUFS))
+        tps = ctx.enter_context(tc.psum_pool(name="tps", bufs=4))
+        ops = ctx.enter_context(tc.psum_pool(name="ops", bufs=4))
+        ctx.enter_context(tc.manual_schedule())
+
+        ident_f = const.tile([P, P], F32)
+        make_identity(nc, ident_f[:])
+        ident_b = const.tile([P, P], BF16)
+        make_identity(nc, ident_b[:])
+        ones = const.tile([P, P], BF16)
+        nc.vector.memset(ones[:], 1.0)
+        b_rows = const.tile([P, FOUT], BF16)
+        nc.vector.memset(b_rows[:], 0.0)
+        perm = const.tile([P, P], BF16)
+        nc.vector.tensor_copy(
+            out=perm[:].rearrange("p (x y r) -> p x y r", x=2, y=8, r=8),
+            in_=ident_b[:].rearrange("p (y x r) -> p x y r", y=8, x=2, r=8),
+        )
+
+        nc.scalar.dma_start(out=b_rows[0:1, :], in_=b.unsqueeze(0))
+
+        x_tiles = {}
+
+        def new_image(i):
+            x_sb = xpool.tile([P, 2, 4096], BF16)
+            x_tiles[i] = x_sb
+
+        def load_half(i, half):
+            src = encoded[i].rearrange("(h p r) d -> p h (r d)", h=2, p=P, r=16)
+            cols = slice(half * 2048, (half + 1) * 2048)
+            for h in range(2):
+                nc.sync.dma_start(out=x_tiles[i][:, h, cols], in_=src[:, h, cols])
+
+        def load_image(i):
+            new_image(i)
+            src = encoded[i].rearrange("(h p r) d -> p h (r d)", h=2, p=P, r=16)
+            nc.sync.dma_start(out=x_tiles[i][:], in_=src)
+
+        w_raw = const.tile([P, 2, 4 * FOUT], BF16)
+        pos_sb = const.tile([P, TILES, FOUT], BF16)
+        pos_src = pos_emb.rearrange("(p t) f -> p t f", t=TILES)
+
+        new_image(0)
+        load_half(0, 0)
+        nc.sync.dma_start(
+            out=w_raw[:], in_=W.rearrange("(c p j) f -> p c (j f)", c=2, p=P, j=4)
+        )
+        load_half(0, 1)
+        nc.sync.dma_start(out=pos_sb[:, 0:4, :], in_=pos_src[:, 0:4, :])
+        new_image(1)
+        load_half(1, 0)
+        nc.sync.dma_start(out=pos_sb[:, 4:8, :], in_=pos_src[:, 4:8, :])
+        load_half(1, 1)
+        for i in range(2, X_BUFS):
+            load_image(i)
+
+        b_bank = ops.tile([P, FOUT], F32, tag="obank")
+        nc.tensor.matmul(out=b_bank[:], lhsT=ones[:], rhs=b_rows[:], start=True, stop=True)
+        b_sb = const.tile([P, FOUT], F32)
+        nc.scalar.copy(out=b_sb[:], in_=b_bank[:])
+        posb = const.tile([P, TILES, FOUT], F32)
+        for xl in range(TILES):
+            nc.gpsimd.tensor_tensor(
+                out=posb[:, xl, :], in0=pos_sb[:, xl, :], in1=b_sb[:], op=ADD
+            )
+
+        def words_of(x_sb, h, xl):
+            return (
+                x_sb[:, h, xl * 512 : (xl + 1) * 512]
+                .bitcast(F32)
+                .rearrange("p (m u) -> p u m", u=2)
+            )
+
+        def sort_group(g):
+            i, half = divmod(g, PER_IMAGE)
+            res = {}
+            if g < FIRST_SORTED:
+                return res
+            for tl in range(NSORT):
+                xl = half * GROUP + tl
+                srt = spool.tile([P, 2, 2, P], F32)
+                for h in range(2):
+                    nc.scalar.copy(out=srt[:, h], in_=words_of(x_tiles[i], h, xl))
+                res[tl] = srt
+            return res
+
+        def transpose_group(g, sorted_tiles):
+            i, half = divmod(g, PER_IMAGE)
+            x_sb = x_tiles[i]
+            grouped = gpool.tile([P, GROUP, 2, 512], BF16, align_bytes=64)
+            for tl in range(GROUP):
+                xl = half * GROUP + tl
+                tbank = tps.tile([P, 512], F32, tag="tbank")
+                for h in range(2):
+                    for u in range(2):
+                        if tl in sorted_tiles:
+                            src_words = sorted_tiles[tl][:, h, u, :]
+                        else:
+                            src_words = words_of(x_sb, h, xl)[:, u, :]
+                        slot = u * 2 + h
+                        nc.tensor.transpose(
+                            out=tbank[:, slot * P : (slot + 1) * P],
+                            in_=src_words,
+                            identity=ident_f[:],
+                        )
+                src = tbank[:].rearrange("p (u a y x) -> p y a x u", u=2, a=32, y=2, x=4)
+                for yh in range(2):
+                    dst = (
+                        grouped[:, tl, yh, :]
+                        .bitcast(F32)
+                        .rearrange("p (a x u) -> p a x u", a=32, x=4, u=2)
+                    )
+                    nc.scalar.copy(out=dst, in_=src[:, yh])
+            return grouped
+
+        def quantise_group(grouped):
+            codes = gpool.tile([P, GROUP, 2 * P], U32, align_bytes=64)
+            scales = gpool.tile([P, GROUP, 2 * P], U8, align_bytes=64)
+            for tl in range(GROUP):
+                nc.vector.quantize_mx(
+                    out=codes[:, tl, :].bitcast(FP8X4),
+                    scales=scales[:, tl, :],
+                    in_=grouped[:, tl].rearrange("p y c -> p (y c)"),
+                )
+            return codes, scales
+
+        w_grouped = const.tile([P, 2, FOUT, 4], BF16, align_bytes=64)
+        w_codes = const.tile([P, 2, FOUT], U32, align_bytes=64)
+        w_scales = const.tile([P, 2, FOUT], U8, align_bytes=64)
+
+        def prepare_w():
+            for c in range(2):
+                for fc in range(4):
+                    if fc % 2 == 0:
+                        w_bank = tps.tile([P, 4, P], F32, tag="tbank")
+                    else:
+                        w_bank = ops.tile([P, 4, P], F32, tag="obank")
+                    for j in range(4):
+                        nc.tensor.matmul(
+                            out=w_bank[:, j, :],
+                            lhsT=perm[:],
+                            rhs=w_raw[:, c, j * FOUT + fc * P : j * FOUT + (fc + 1) * P],
+                            start=True,
+                            stop=True,
+                        )
+                    dst = w_grouped[:, c, fc * P : (fc + 1) * P, :]
+                    src = w_bank[:].rearrange("p j f -> p f j")
+                    if fc % 2 == 0:
+                        nc.scalar.copy(out=dst, in_=src)
+                    else:
+                        nc.vector.tensor_copy(out=dst, in_=src)
+                nc.vector.quantize_mx(
+                    out=w_codes[:, c, :].bitcast(FP8X4),
+                    scales=w_scales[:, c, :],
+                    in_=w_grouped[:, c].rearrange("p f j -> p (f j)"),
+                )
+
+        def multiply_group(g, codes, scales):
+            i, half = divmod(g, PER_IMAGE)
+            o_sb = opool.tile([P, GROUP, FOUT], F32)
+            dst = out[i].rearrange("(p t) f -> p t f", t=TILES)
+            for tl in range(GROUP):
+                xl = half * GROUP + tl
+                obank = ops.tile([P, FOUT], F32, tag="obank")
+                for yh in range(2):
+                    cols = slice(yh * P, (yh + 1) * P)
+                    nc.tensor.matmul_mx(
+                        out=obank[:],
+                        lhsT=codes[:, tl, cols].bitcast(FP8X4),
+                        lhsT_scale=scales[:, tl, cols],
+                        rhs=w_codes[:, yh, :].bitcast(FP8X4),
+                        rhs_scale=w_scales[:, yh, :],
+                        start=(yh == 0),
+                        stop=(yh == 1),
+                    )
+                nc.vector.tensor_tensor(
+                    out=o_sb[:, tl, :], in0=obank[:], in1=posb[:, xl, :], op=ADD
+                )
+                if g == GROUPS - 1:
+                    nc.sync.dma_start(out=dst[:, xl : xl + 1, :], in_=o_sb[:, tl : tl + 1, :])
+            if g < GROUPS - 1:
+                nc.sync.dma_start(
+                    out=dst[:, half * GROUP : (half + 1) * GROUP, :], in_=o_sb[:]
+                )
+
+        grouped_of = {0: transpose_group(0, sort_group(0))}
+        quantised_of = {0: quantise_group(grouped_of[0])}
+        prepare_w()
+        sorted_of = {1: sort_group(1)}
+        for g in range(GROUPS):
+            if g + 1 < GROUPS:
+                grouped_of[g + 1] = transpose_group(g + 1, sorted_of[g + 1])
+                i_done, half_done = divmod(g + 1, PER_IMAGE)
+                if half_done == PER_IMAGE - 1 and i_done + X_BUFS < IMAGES:
+                    load_image(i_done + X_BUFS)
+            if g + 2 < GROUPS:
+                sorted_of[g + 2] = sort_group(g + 2)
+            if g > 0:
+                quantised_of[g] = quantise_group(grouped_of[g])
+            codes, scales = quantised_of[g]
+            multiply_group(g, codes, scales)

@@ -21,7 +21,7 @@ GROUPS = IMAGES * PER_IMAGE
 FOUT = 512
 X_BUFS = 4
 O_BUFS = 6
-NSORT = 0
+NSORT = 3
 FIRST_SORTED = 2
 
 
@@ -41,17 +41,15 @@ def tile_resampling_t_kernel(tc, encoded, W, b, pos_emb, out):
         make_identity(nc, ident_f[:])
         ident_b = const.tile([P, P], BF16)
         make_identity(nc, ident_b[:])
-        ones = const.tile([P, P], BF16)
-        nc.vector.memset(ones[:], 1.0)
         b_rows = const.tile([P, FOUT], BF16)
         nc.vector.memset(b_rows[:], 0.0)
+        ones = const.tile([P, P], BF16)
+        nc.vector.memset(ones[:], 1.0)
         perm = const.tile([P, P], BF16)
         nc.vector.tensor_copy(
             out=perm[:].rearrange("p (x y r) -> p x y r", x=2, y=8, r=8),
             in_=ident_b[:].rearrange("p (y x r) -> p x y r", y=8, x=2, r=8),
         )
-
-        nc.scalar.dma_start(out=b_rows[0:1, :], in_=b.unsqueeze(0))
 
         x_tiles = {}
 
@@ -76,6 +74,7 @@ def tile_resampling_t_kernel(tc, encoded, W, b, pos_emb, out):
 
         new_image(0)
         load_half(0, 0)
+        nc.sync.dma_start(out=b_rows[0:1, :], in_=b.unsqueeze(0))
         nc.sync.dma_start(
             out=w_raw[:], in_=W.rearrange("(c p j) f -> p c (j f)", c=2, p=P, j=4)
         )
@@ -88,15 +87,17 @@ def tile_resampling_t_kernel(tc, encoded, W, b, pos_emb, out):
         for i in range(2, X_BUFS):
             load_image(i)
 
-        b_bank = ops.tile([P, FOUT], F32, tag="obank")
-        nc.tensor.matmul(out=b_bank[:], lhsT=ones[:], rhs=b_rows[:], start=True, stop=True)
-        b_sb = const.tile([P, FOUT], F32)
-        nc.scalar.copy(out=b_sb[:], in_=b_bank[:])
         posb = const.tile([P, TILES, FOUT], F32)
-        for xl in range(TILES):
-            nc.gpsimd.tensor_tensor(
-                out=posb[:, xl, :], in0=pos_sb[:, xl, :], in1=b_sb[:], op=ADD
-            )
+
+        def prepare_posb():
+            b_bank = ops.tile([P, FOUT], F32, tag="obank")
+            nc.tensor.matmul(out=b_bank[:], lhsT=ones[:], rhs=b_rows[:], start=True, stop=True)
+            b_sb = const.tile([P, FOUT], F32)
+            nc.scalar.copy(out=b_sb[:], in_=b_bank[:])
+            for xl in range(TILES):
+                nc.gpsimd.tensor_tensor(
+                    out=posb[:, xl, :], in0=pos_sb[:, xl, :], in1=b_sb[:], op=ADD
+                )
 
         def words_of(x_sb, h, xl):
             return (
@@ -147,16 +148,17 @@ def tile_resampling_t_kernel(tc, encoded, W, b, pos_emb, out):
                     nc.scalar.copy(out=dst, in_=src[:, yh])
             return grouped
 
-        def quantise_group(grouped):
+        def new_codes():
             codes = gpool.tile([P, GROUP, 2 * P], U32, align_bytes=64)
             scales = gpool.tile([P, GROUP, 2 * P], U8, align_bytes=64)
-            for tl in range(GROUP):
-                nc.vector.quantize_mx(
-                    out=codes[:, tl, :].bitcast(FP8X4),
-                    scales=scales[:, tl, :],
-                    in_=grouped[:, tl].rearrange("p y c -> p (y c)"),
-                )
             return codes, scales
+
+        def quantise_tile(grouped, codes, scales, tl):
+            nc.vector.quantize_mx(
+                out=codes[:, tl, :].bitcast(FP8X4),
+                scales=scales[:, tl, :],
+                in_=grouped[:, tl].rearrange("p y c -> p (y c)"),
+            )
 
         w_grouped = const.tile([P, 2, FOUT, 4], BF16, align_bytes=64)
         w_codes = const.tile([P, 2, FOUT], U32, align_bytes=64)
@@ -189,7 +191,7 @@ def tile_resampling_t_kernel(tc, encoded, W, b, pos_emb, out):
                     in_=w_grouped[:, c].rearrange("p f j -> p (f j)"),
                 )
 
-        def multiply_group(g, codes, scales):
+        def multiply_group(g, codes, scales, next_grouped, next_codes, next_scales):
             i, half = divmod(g, PER_IMAGE)
             o_sb = opool.tile([P, GROUP, FOUT], F32)
             dst = out[i].rearrange("(p t) f -> p t f", t=TILES)
@@ -212,24 +214,29 @@ def tile_resampling_t_kernel(tc, encoded, W, b, pos_emb, out):
                 )
                 if g == GROUPS - 1:
                     nc.sync.dma_start(out=dst[:, xl : xl + 1, :], in_=o_sb[:, tl : tl + 1, :])
+                else:
+                    quantise_tile(next_grouped, next_codes, next_scales, tl)
             if g < GROUPS - 1:
                 nc.sync.dma_start(
                     out=dst[:, half * GROUP : (half + 1) * GROUP, :], in_=o_sb[:]
                 )
 
-        grouped_of = {0: transpose_group(0, sort_group(0))}
-        quantised_of = {0: quantise_group(grouped_of[0])}
+        grouped = transpose_group(0, sort_group(0))
+        codes, scales = new_codes()
+        for tl in range(GROUP):
+            quantise_tile(grouped, codes, scales, tl)
+        prepare_posb()
         prepare_w()
-        sorted_of = {1: sort_group(1)}
+        sorted_next = sort_group(1)
         for g in range(GROUPS):
+            next_grouped, next_codes, next_scales = None, None, None
             if g + 1 < GROUPS:
-                grouped_of[g + 1] = transpose_group(g + 1, sorted_of[g + 1])
+                next_grouped = transpose_group(g + 1, sorted_next)
+                next_codes, next_scales = new_codes()
                 i_done, half_done = divmod(g + 1, PER_IMAGE)
                 if half_done == PER_IMAGE - 1 and i_done + X_BUFS < IMAGES:
                     load_image(i_done + X_BUFS)
             if g + 2 < GROUPS:
-                sorted_of[g + 2] = sort_group(g + 2)
-            if g > 0:
-                quantised_of[g] = quantise_group(grouped_of[g])
-            codes, scales = quantised_of[g]
-            multiply_group(g, codes, scales)
+                sorted_next = sort_group(g + 2)
+            multiply_group(g, codes, scales, next_grouped, next_codes, next_scales)
+            codes, scales = next_codes, next_scales

@@ -21,7 +21,8 @@ GROUPS = IMAGES * PER_IMAGE
 FOUT = 512
 X_BUFS = 4
 O_BUFS = 6
-NSORT = 3
+QTILES = 2
+NSORT = 2
 FIRST_SORTED = 2
 
 
@@ -54,19 +55,20 @@ def tile_resampling_t_kernel(tc, encoded, W, b, pos_emb, out):
         x_tiles = {}
 
         def new_image(i):
-            x_sb = xpool.tile([P, 2, 4096], BF16)
+            x_sb = xpool.tile([P, 2 * 4096], BF16)
             x_tiles[i] = x_sb
 
         def load_half(i, half):
             src = encoded[i].rearrange("(h p r) d -> p h (r d)", h=2, p=P, r=16)
             cols = slice(half * 2048, (half + 1) * 2048)
+            dst = x_tiles[i][:].rearrange("p (h c) -> p h c", h=2)
             for h in range(2):
-                nc.sync.dma_start(out=x_tiles[i][:, h, cols], in_=src[:, h, cols])
+                nc.sync.dma_start(out=dst[:, h, cols], in_=src[:, h, cols])
 
         def load_image(i):
             new_image(i)
             src = encoded[i].rearrange("(h p r) d -> p h (r d)", h=2, p=P, r=16)
-            nc.sync.dma_start(out=x_tiles[i][:], in_=src)
+            nc.sync.dma_start(out=x_tiles[i][:].rearrange("p (h c) -> p h c", h=2), in_=src)
 
         w_raw = const.tile([P, 2, 4 * FOUT], BF16)
         pos_sb = const.tile([P, TILES, FOUT], BF16)
@@ -99,11 +101,9 @@ def tile_resampling_t_kernel(tc, encoded, W, b, pos_emb, out):
                     out=posb[:, xl, :], in0=pos_sb[:, xl, :], in1=b_sb[:], op=ADD
                 )
 
-        def words_of(x_sb, h, xl):
-            return (
-                x_sb[:, h, xl * 512 : (xl + 1) * 512]
-                .bitcast(F32)
-                .rearrange("p (m u) -> p u m", u=2)
+        def words_of(x_sb):
+            return x_sb[:].bitcast(F32).rearrange(
+                "p (h t m u) -> p h t u m", h=2, t=TILES, m=P, u=2
             )
 
         def sort_group(g):
@@ -114,15 +114,14 @@ def tile_resampling_t_kernel(tc, encoded, W, b, pos_emb, out):
             for tl in range(NSORT):
                 xl = half * GROUP + tl
                 srt = spool.tile([P, 2, 2, P], F32)
-                for h in range(2):
-                    nc.scalar.copy(out=srt[:, h], in_=words_of(x_tiles[i], h, xl))
+                nc.scalar.copy(out=srt[:], in_=words_of(x_tiles[i])[:, :, xl, :, :])
                 res[tl] = srt
             return res
 
         def transpose_group(g, sorted_tiles):
             i, half = divmod(g, PER_IMAGE)
             x_sb = x_tiles[i]
-            grouped = gpool.tile([P, GROUP, 2, 512], BF16, align_bytes=64)
+            grouped = gpool.tile([P, GROUP * 1024], BF16, align_bytes=64)
             for tl in range(GROUP):
                 xl = half * GROUP + tl
                 tbank = tps.tile([P, 512], F32, tag="tbank")
@@ -131,7 +130,7 @@ def tile_resampling_t_kernel(tc, encoded, W, b, pos_emb, out):
                         if tl in sorted_tiles:
                             src_words = sorted_tiles[tl][:, h, u, :]
                         else:
-                            src_words = words_of(x_sb, h, xl)[:, u, :]
+                            src_words = words_of(x_sb)[:, h, xl, u, :]
                         slot = u * 2 + h
                         nc.tensor.transpose(
                             out=tbank[:, slot * P : (slot + 1) * P],
@@ -139,25 +138,25 @@ def tile_resampling_t_kernel(tc, encoded, W, b, pos_emb, out):
                             identity=ident_f[:],
                         )
                 src = tbank[:].rearrange("p (u a y x) -> p y a x u", u=2, a=32, y=2, x=4)
-                for yh in range(2):
-                    dst = (
-                        grouped[:, tl, yh, :]
-                        .bitcast(F32)
-                        .rearrange("p (a x u) -> p a x u", a=32, x=4, u=2)
-                    )
-                    nc.scalar.copy(out=dst, in_=src[:, yh])
+                dst = (
+                    grouped[:, tl * 1024 : (tl + 1) * 1024]
+                    .bitcast(F32)
+                    .rearrange("p (y a x u) -> p y a x u", y=2, a=32, x=4, u=2)
+                )
+                nc.scalar.copy(out=dst, in_=src)
             return grouped
 
         def new_codes():
-            codes = gpool.tile([P, GROUP, 2 * P], U32, align_bytes=64)
-            scales = gpool.tile([P, GROUP, 2 * P], U8, align_bytes=64)
+            codes = gpool.tile([P, GROUP * 2 * P], U32, align_bytes=64)
+            scales = gpool.tile([P, GROUP * 2 * P], U8, align_bytes=64)
             return codes, scales
 
-        def quantise_tile(grouped, codes, scales, tl):
+        def quantise_tiles(grouped, codes, scales, first):
+            words = slice(first * 2 * P, (first + QTILES) * 2 * P)
             nc.vector.quantize_mx(
-                out=codes[:, tl, :].bitcast(FP8X4),
-                scales=scales[:, tl, :],
-                in_=grouped[:, tl].rearrange("p y c -> p (y c)"),
+                out=codes[:, words].bitcast(FP8X4),
+                scales=scales[:, words],
+                in_=grouped[:, first * 1024 : (first + QTILES) * 1024],
             )
 
         w_grouped = const.tile([P, 2, FOUT, 4], BF16, align_bytes=64)
@@ -199,11 +198,11 @@ def tile_resampling_t_kernel(tc, encoded, W, b, pos_emb, out):
                 xl = half * GROUP + tl
                 obank = ops.tile([P, FOUT], F32, tag="obank")
                 for yh in range(2):
-                    cols = slice(yh * P, (yh + 1) * P)
+                    cols = slice((tl * 2 + yh) * P, (tl * 2 + yh + 1) * P)
                     nc.tensor.matmul_mx(
                         out=obank[:],
-                        lhsT=codes[:, tl, cols].bitcast(FP8X4),
-                        lhsT_scale=scales[:, tl, cols],
+                        lhsT=codes[:, cols].bitcast(FP8X4),
+                        lhsT_scale=scales[:, cols],
                         rhs=w_codes[:, yh, :].bitcast(FP8X4),
                         rhs_scale=w_scales[:, yh, :],
                         start=(yh == 0),
@@ -214,8 +213,8 @@ def tile_resampling_t_kernel(tc, encoded, W, b, pos_emb, out):
                 )
                 if g == GROUPS - 1:
                     nc.sync.dma_start(out=dst[:, xl : xl + 1, :], in_=o_sb[:, tl : tl + 1, :])
-                else:
-                    quantise_tile(next_grouped, next_codes, next_scales, tl)
+                elif tl % QTILES == QTILES - 1:
+                    quantise_tiles(next_grouped, next_codes, next_scales, tl + 1 - QTILES)
             if g < GROUPS - 1:
                 nc.sync.dma_start(
                     out=dst[:, half * GROUP : (half + 1) * GROUP, :], in_=o_sb[:]
@@ -223,8 +222,8 @@ def tile_resampling_t_kernel(tc, encoded, W, b, pos_emb, out):
 
         grouped = transpose_group(0, sort_group(0))
         codes, scales = new_codes()
-        for tl in range(GROUP):
-            quantise_tile(grouped, codes, scales, tl)
+        for tl in range(0, GROUP, QTILES):
+            quantise_tiles(grouped, codes, scales, tl)
         prepare_posb()
         prepare_w()
         sorted_next = sort_group(1)

@@ -24,6 +24,7 @@ O_BUFS = 6
 QTILES = 2
 NSORT = 2
 FIRST_SORTED = 2
+STORE_AFTER_TILE = 1
 
 
 def tile_resampling_t_kernel(tc, encoded, W, b, pos_emb, out):
@@ -118,6 +119,13 @@ def tile_resampling_t_kernel(tc, encoded, W, b, pos_emb, out):
                 res[tl] = srt
             return res
 
+        store_of = {}
+
+        def trigger_store(g):
+            if g in store_of:
+                dst, src = store_of[g]
+                nc.scalar.dma_start(out=dst, in_=src)
+
         def transpose_group(g, sorted_tiles):
             i, half = divmod(g, PER_IMAGE)
             x_sb = x_tiles[i]
@@ -144,6 +152,8 @@ def tile_resampling_t_kernel(tc, encoded, W, b, pos_emb, out):
                     .rearrange("p (y a x u) -> p y a x u", y=2, a=32, x=4, u=2)
                 )
                 nc.scalar.copy(out=dst, in_=src)
+                if tl == STORE_AFTER_TILE:
+                    trigger_store(g - 2)
             return grouped
 
         def new_codes():
@@ -216,9 +226,7 @@ def tile_resampling_t_kernel(tc, encoded, W, b, pos_emb, out):
                 elif tl % QTILES == QTILES - 1:
                     quantise_tiles(next_grouped, next_codes, next_scales, tl + 1 - QTILES)
             if g < GROUPS - 1:
-                nc.sync.dma_start(
-                    out=dst[:, half * GROUP : (half + 1) * GROUP, :], in_=o_sb[:]
-                )
+                store_of[g] = (dst[:, half * GROUP : (half + 1) * GROUP, :], o_sb[:])
 
         grouped = transpose_group(0, sort_group(0))
         codes, scales = new_codes()
@@ -235,6 +243,8 @@ def tile_resampling_t_kernel(tc, encoded, W, b, pos_emb, out):
                 i_done, half_done = divmod(g + 1, PER_IMAGE)
                 if half_done == PER_IMAGE - 1 and i_done + X_BUFS < IMAGES:
                     load_image(i_done + X_BUFS)
+            else:
+                trigger_store(g - 1)
             if g + 2 < GROUPS:
                 sorted_next = sort_group(g + 2)
             multiply_group(g, codes, scales, next_grouped, next_codes, next_scales)

@@ -24,7 +24,7 @@ O_BUFS = 6
 QTILES = 2
 NSORT = 2
 FIRST_SORTED = 2
-STORE_AFTER_TILE = 1
+SORT_AHEAD = 3
 
 
 def tile_resampling_t_kernel(tc, encoded, W, b, pos_emb, out):
@@ -32,7 +32,7 @@ def tile_resampling_t_kernel(tc, encoded, W, b, pos_emb, out):
     with ExitStack() as ctx:
         const = ctx.enter_context(tc.tile_pool(name="const", bufs=1))
         xpool = ctx.enter_context(tc.tile_pool(name="xpool", bufs=X_BUFS))
-        spool = ctx.enter_context(tc.tile_pool(name="spool", bufs=2 * NSORT)) if NSORT else None
+        spool = ctx.enter_context(tc.tile_pool(name="spool", bufs=SORT_AHEAD * NSORT))
         gpool = ctx.enter_context(tc.tile_pool(name="gpool", bufs=3))
         opool = ctx.enter_context(tc.tile_pool(name="opool", bufs=O_BUFS))
         tps = ctx.enter_context(tc.psum_pool(name="tps", bufs=4))
@@ -119,13 +119,6 @@ def tile_resampling_t_kernel(tc, encoded, W, b, pos_emb, out):
                 res[tl] = srt
             return res
 
-        store_of = {}
-
-        def trigger_store(g):
-            if g in store_of:
-                dst, src = store_of[g]
-                nc.scalar.dma_start(out=dst, in_=src)
-
         def transpose_group(g, sorted_tiles):
             i, half = divmod(g, PER_IMAGE)
             x_sb = x_tiles[i]
@@ -152,8 +145,6 @@ def tile_resampling_t_kernel(tc, encoded, W, b, pos_emb, out):
                     .rearrange("p (y a x u) -> p y a x u", y=2, a=32, x=4, u=2)
                 )
                 nc.scalar.copy(out=dst, in_=src)
-                if tl == STORE_AFTER_TILE:
-                    trigger_store(g - 2)
             return grouped
 
         def new_codes():
@@ -226,7 +217,9 @@ def tile_resampling_t_kernel(tc, encoded, W, b, pos_emb, out):
                 elif tl % QTILES == QTILES - 1:
                     quantise_tiles(next_grouped, next_codes, next_scales, tl + 1 - QTILES)
             if g < GROUPS - 1:
-                store_of[g] = (dst[:, half * GROUP : (half + 1) * GROUP, :], o_sb[:])
+                nc.sync.dma_start(
+                    out=dst[:, half * GROUP : (half + 1) * GROUP, :], in_=o_sb[:]
+                )
 
         grouped = transpose_group(0, sort_group(0))
         codes, scales = new_codes()
@@ -234,18 +227,19 @@ def tile_resampling_t_kernel(tc, encoded, W, b, pos_emb, out):
             quantise_tiles(grouped, codes, scales, tl)
         prepare_posb()
         prepare_w()
-        sorted_next = sort_group(1)
+        sorted_of = {1: sort_group(1)}
+        next_to_sort = 2
         for g in range(GROUPS):
             next_grouped, next_codes, next_scales = None, None, None
             if g + 1 < GROUPS:
-                next_grouped = transpose_group(g + 1, sorted_next)
+                next_grouped = transpose_group(g + 1, sorted_of[g + 1])
                 next_codes, next_scales = new_codes()
                 i_done, half_done = divmod(g + 1, PER_IMAGE)
                 if half_done == PER_IMAGE - 1 and i_done + X_BUFS < IMAGES:
                     load_image(i_done + X_BUFS)
-            else:
-                trigger_store(g - 1)
-            if g + 2 < GROUPS:
-                sorted_next = sort_group(g + 2)
+            ahead = SORT_AHEAD if g >= 2 else SORT_AHEAD - 1
+            for k in range(next_to_sort, min(g + ahead, GROUPS - 1) + 1):
+                sorted_of[k] = sort_group(k)
+                next_to_sort = k + 1
             multiply_group(g, codes, scales, next_grouped, next_codes, next_scales)
             codes, scales = next_codes, next_scales

@@ -22,7 +22,8 @@ FOUT = 512
 X_BUFS = 4
 O_BUFS = 6
 QTILES = 2
-NSORT = 2
+TAPER = 2
+NSORT = 3
 FIRST_SORTED = 2
 SORT_AHEAD = 3
 
@@ -212,11 +213,11 @@ def tile_resampling_t_kernel(tc, encoded, W, b, pos_emb, out):
                 nc.vector.tensor_tensor(
                     out=o_sb[:, tl, :], in0=obank[:], in1=posb[:, xl, :], op=ADD
                 )
-                if g == GROUPS - 1:
+                if g >= GROUPS - TAPER:
                     nc.sync.dma_start(out=dst[:, xl : xl + 1, :], in_=o_sb[:, tl : tl + 1, :])
-                elif tl % QTILES == QTILES - 1:
+                if g < GROUPS - 1 and tl % QTILES == QTILES - 1:
                     quantise_tiles(next_grouped, next_codes, next_scales, tl + 1 - QTILES)
-            if g < GROUPS - 1:
+            if g < GROUPS - TAPER:
                 nc.sync.dma_start(
                     out=dst[:, half * GROUP : (half + 1) * GROUP, :], in_=o_sb[:]
                 )

@@ -22,6 +22,7 @@ FOUT = 512
 X_BUFS = 4
 O_BUFS = 6
 QTILES = 2
+WARM = 6
 TAPER = 2
 NSORT = 3
 FIRST_SORTED = 2
@@ -48,6 +49,13 @@ def tile_resampling_t_kernel(tc, encoded, W, b, pos_emb, out):
         nc.vector.memset(b_rows[:], 0.0)
         ones = const.tile([P, P], BF16)
         nc.vector.memset(ones[:], 1.0)
+        warm_rhs = const.tile([P, FOUT], BF16)
+        nc.vector.memset(warm_rhs[:], 0.0)
+        warm_bank = tps.tile([P, FOUT], F32, tag="tbank")
+        for n in range(WARM):
+            nc.tensor.matmul(
+                out=warm_bank[:], lhsT=ones[:], rhs=warm_rhs[:], start=True, stop=True
+            )
         perm = const.tile([P, P], BF16)
         nc.vector.tensor_copy(
             out=perm[:].rearrange("p (x y r) -> p x y r", x=2, y=8, r=8),
@@ -196,27 +204,32 @@ def tile_resampling_t_kernel(tc, encoded, W, b, pos_emb, out):
             i, half = divmod(g, PER_IMAGE)
             o_sb = opool.tile([P, GROUP, FOUT], F32)
             dst = out[i].rearrange("(p t) f -> p t f", t=TILES)
-            for tl in range(GROUP):
-                xl = half * GROUP + tl
-                obank = ops.tile([P, FOUT], F32, tag="obank")
-                for yh in range(2):
-                    cols = slice((tl * 2 + yh) * P, (tl * 2 + yh + 1) * P)
-                    nc.tensor.matmul_mx(
-                        out=obank[:],
-                        lhsT=codes[:, cols].bitcast(FP8X4),
-                        lhsT_scale=scales[:, cols],
-                        rhs=w_codes[:, yh, :].bitcast(FP8X4),
-                        rhs_scale=w_scales[:, yh, :],
-                        start=(yh == 0),
-                        stop=(yh == 1),
+            early = QTILES if g == GROUPS - 2 else 0
+            for tl in range(-early, GROUP):
+                if tl >= 0:
+                    xl = half * GROUP + tl
+                    obank = ops.tile([P, FOUT], F32, tag="obank")
+                    for yh in range(2):
+                        cols = slice((tl * 2 + yh) * P, (tl * 2 + yh + 1) * P)
+                        nc.tensor.matmul_mx(
+                            out=obank[:],
+                            lhsT=codes[:, cols].bitcast(FP8X4),
+                            lhsT_scale=scales[:, cols],
+                            rhs=w_codes[:, yh, :].bitcast(FP8X4),
+                            rhs_scale=w_scales[:, yh, :],
+                            start=(yh == 0),
+                            stop=(yh == 1),
+                        )
+                    nc.vector.tensor_tensor(
+                        out=o_sb[:, tl, :], in0=obank[:], in1=posb[:, xl, :], op=ADD
                     )
-                nc.vector.tensor_tensor(
-                    out=o_sb[:, tl, :], in0=obank[:], in1=posb[:, xl, :], op=ADD
-                )
-                if g >= GROUPS - TAPER:
-                    nc.sync.dma_start(out=dst[:, xl : xl + 1, :], in_=o_sb[:, tl : tl + 1, :])
-                if g < GROUPS - 1 and tl % QTILES == QTILES - 1:
-                    quantise_tiles(next_grouped, next_codes, next_scales, tl + 1 - QTILES)
+                    if g >= GROUPS - TAPER:
+                        nc.sync.dma_start(
+                            out=dst[:, xl : xl + 1, :], in_=o_sb[:, tl : tl + 1, :]
+                        )
+                first = tl + early + 1 - QTILES
+                if g < GROUPS - 1 and first % QTILES == 0 and 0 <= first < GROUP:
+                    quantise_tiles(next_grouped, next_codes, next_scales, first)
             if g < GROUPS - TAPER:
                 nc.sync.dma_start(
                     out=dst[:, half * GROUP : (half + 1) * GROUP, :], in_=o_sb[:]

@@ -22,7 +22,6 @@ FOUT = 512
 X_BUFS = 4
 O_BUFS = 6
 QTILES = 2
-WARM = 6
 TAPER = 2
 NSORT = 3
 FIRST_SORTED = 2
@@ -39,7 +38,6 @@ def tile_resampling_t_kernel(tc, encoded, W, b, pos_emb, out):
         opool = ctx.enter_context(tc.tile_pool(name="opool", bufs=O_BUFS))
         tps = ctx.enter_context(tc.psum_pool(name="tps", bufs=4))
         ops = ctx.enter_context(tc.psum_pool(name="ops", bufs=4))
-        ctx.enter_context(tc.manual_schedule())
 
         ident_f = const.tile([P, P], F32)
         make_identity(nc, ident_f[:])
@@ -49,13 +47,6 @@ def tile_resampling_t_kernel(tc, encoded, W, b, pos_emb, out):
         nc.vector.memset(b_rows[:], 0.0)
         ones = const.tile([P, P], BF16)
         nc.vector.memset(ones[:], 1.0)
-        warm_rhs = const.tile([P, FOUT], BF16)
-        nc.vector.memset(warm_rhs[:], 0.0)
-        warm_bank = tps.tile([P, FOUT], F32, tag="tbank")
-        for n in range(WARM):
-            nc.tensor.matmul(
-                out=warm_bank[:], lhsT=ones[:], rhs=warm_rhs[:], start=True, stop=True
-            )
         perm = const.tile([P, P], BF16)
         nc.vector.tensor_copy(
             out=perm[:].rearrange("p (x y r) -> p x y r", x=2, y=8, r=8),
@@ -204,32 +195,27 @@ def tile_resampling_t_kernel(tc, encoded, W, b, pos_emb, out):
             i, half = divmod(g, PER_IMAGE)
             o_sb = opool.tile([P, GROUP, FOUT], F32)
             dst = out[i].rearrange("(p t) f -> p t f", t=TILES)
-            early = QTILES if g == GROUPS - 2 else 0
-            for tl in range(-early, GROUP):
-                if tl >= 0:
-                    xl = half * GROUP + tl
-                    obank = ops.tile([P, FOUT], F32, tag="obank")
-                    for yh in range(2):
-                        cols = slice((tl * 2 + yh) * P, (tl * 2 + yh + 1) * P)
-                        nc.tensor.matmul_mx(
-                            out=obank[:],
-                            lhsT=codes[:, cols].bitcast(FP8X4),
-                            lhsT_scale=scales[:, cols],
-                            rhs=w_codes[:, yh, :].bitcast(FP8X4),
-                            rhs_scale=w_scales[:, yh, :],
-                            start=(yh == 0),
-                            stop=(yh == 1),
-                        )
-                    nc.vector.tensor_tensor(
-                        out=o_sb[:, tl, :], in0=obank[:], in1=posb[:, xl, :], op=ADD
+            for tl in range(GROUP):
+                xl = half * GROUP + tl
+                obank = ops.tile([P, FOUT], F32, tag="obank")
+                for yh in range(2):
+                    cols = slice((tl * 2 + yh) * P, (tl * 2 + yh + 1) * P)
+                    nc.tensor.matmul_mx(
+                        out=obank[:],
+                        lhsT=codes[:, cols].bitcast(FP8X4),
+                        lhsT_scale=scales[:, cols],
+                        rhs=w_codes[:, yh, :].bitcast(FP8X4),
+                        rhs_scale=w_scales[:, yh, :],
+                        start=(yh == 0),
+                        stop=(yh == 1),
                     )
-                    if g >= GROUPS - TAPER:
-                        nc.sync.dma_start(
-                            out=dst[:, xl : xl + 1, :], in_=o_sb[:, tl : tl + 1, :]
-                        )
-                first = tl + early + 1 - QTILES
-                if g < GROUPS - 1 and first % QTILES == 0 and 0 <= first < GROUP:
-                    quantise_tiles(next_grouped, next_codes, next_scales, first)
+                nc.vector.tensor_tensor(
+                    out=o_sb[:, tl, :], in0=obank[:], in1=posb[:, xl, :], op=ADD
+                )
+                if g >= GROUPS - TAPER:
+                    nc.sync.dma_start(out=dst[:, xl : xl + 1, :], in_=o_sb[:, tl : tl + 1, :])
+                if g < GROUPS - 1 and tl % QTILES == QTILES - 1:
+                    quantise_tiles(next_grouped, next_codes, next_scales, tl + 1 - QTILES)
             if g < GROUPS - TAPER:
                 nc.sync.dma_start(
                     out=dst[:, half * GROUP : (half + 1) * GROUP, :], in_=o_sb[:]

from contextlib import ExitStack

import concourse.mybir as mybir
from concourse.masks import make_identity

FLOPS = 2 * 8 * 1024 * 1024 * 512

BF16 = mybir.dt.bfloat16
F32 = mybir.dt.float32
U32 = mybir.dt.uint32
U8 = mybir.dt.uint8
FP8X4 = mybir.dt.float8_e4m3fn_x4
ADD = mybir.AluOpType.add

P = 128
IMAGES = 8
TILES = 8
GROUP = 4
PER_IMAGE = TILES // GROUP
GROUPS = IMAGES * PER_IMAGE
FOUT = 512
X_BUFS = 4
O_BUFS = 6
QTILES = 2
TAPER = 2
NSORT = 3
FIRST_SORTED = 2
SORT_AHEAD = 3


def tile_resampling_t_kernel(tc, encoded, W, b, pos_emb, out):
    nc = tc.nc
    with ExitStack() as ctx:
        const = ctx.enter_context(tc.tile_pool(name="const", bufs=1))
        xpool = ctx.enter_context(tc.tile_pool(name="xpool", bufs=X_BUFS))
        spool = ctx.enter_context(tc.tile_pool(name="spool", bufs=SORT_AHEAD * NSORT))
        gpool = ctx.enter_context(tc.tile_pool(name="gpool", bufs=3))
        opool = ctx.enter_context(tc.tile_pool(name="opool", bufs=O_BUFS))
        tps = ctx.enter_context(tc.psum_pool(name="tps", bufs=4))
        ops = ctx.enter_context(tc.psum_pool(name="ops", bufs=4))

        ident_f = const.tile([P, P], F32)
        make_identity(nc, ident_f[:])
        ident_b = const.tile([P, P], BF16)
        make_identity(nc, ident_b[:])
        b_rows = const.tile([P, FOUT], BF16)
        nc.vector.memset(b_rows[:], 0.0)
        ones = const.tile([P, P], BF16)
        nc.vector.memset(ones[:], 1.0)
        perm = const.tile([P, P], BF16)
        nc.vector.tensor_copy(
            out=perm[:].rearrange("p (x y r) -> p x y r", x=2, y=8, r=8),
            in_=ident_b[:].rearrange("p (y x r) -> p x y r", y=8, x=2, r=8),
        )

        x_tiles = {}

        def new_image(i):
            x_sb = xpool.tile([P, 2 * 4096], BF16)
            x_tiles[i] = x_sb

        def load_half(i, half):
            src = encoded[i].rearrange("(h p r) d -> p h (r d)", h=2, p=P, r=16)
            cols = slice(half * 2048, (half + 1) * 2048)
            dst = x_tiles[i][:].rearrange("p (h c) -> p h c", h=2)
            for h in range(2):
                nc.sync.dma_start(out=dst[:, h, cols], in_=src[:, h, cols])

        def load_image(i):
            new_image(i)
            src = encoded[i].rearrange("(h p r) d -> p h (r d)", h=2, p=P, r=16)
            nc.sync.dma_start(out=x_tiles[i][:].rearrange("p (h c) -> p h c", h=2), in_=src)

        w_raw = const.tile([P, 2, 4 * FOUT], BF16)
        pos_sb = const.tile([P, TILES, FOUT], BF16)
        pos_src = pos_emb.rearrange("(p t) f -> p t f", t=TILES)

        new_image(0)
        load_half(0, 0)
        nc.sync.dma_start(out=b_rows[0:1, :], in_=b.unsqueeze(0))
        nc.sync.dma_start(
            out=w_raw[:], in_=W.rearrange("(c p j) f -> p c (j f)", c=2, p=P, j=4)
        )
        load_half(0, 1)
        nc.sync.dma_start(out=pos_sb[:, 0:4, :], in_=pos_src[:, 0:4, :])
        new_image(1)
        load_half(1, 0)
        nc.sync.dma_start(out=pos_sb[:, 4:8, :], in_=pos_src[:, 4:8, :])
        load_half(1, 1)
        for i in range(2, X_BUFS):
            load_image(i)

        posb = const.tile([P, TILES, FOUT], F32)

        def prepare_posb():
            b_bank = ops.tile([P, FOUT], F32, tag="obank")
            nc.tensor.matmul(out=b_bank[:], lhsT=ones[:], rhs=b_rows[:], start=True, stop=True)
            b_sb = const.tile([P, FOUT], F32)
            nc.scalar.copy(out=b_sb[:], in_=b_bank[:])
            for xl in range(TILES):
                nc.gpsimd.tensor_tensor(
                    out=posb[:, xl, :], in0=pos_sb[:, xl, :], in1=b_sb[:], op=ADD
                )

        def words_of(x_sb):
            return x_sb[:].bitcast(F32).rearrange(
                "p (h t m u) -> p h t u m", h=2, t=TILES, m=P, u=2
            )

        def sort_group(g):
            i, half = divmod(g, PER_IMAGE)
            res = {}
            if g < FIRST_SORTED:
                return res
            for tl in range(NSORT):
                xl = half * GROUP + tl
                srt = spool.tile([P, 2, 2, P], F32)
                nc.scalar.copy(out=srt[:], in_=words_of(x_tiles[i])[:, :, xl, :, :])
                res[tl] = srt
            return res

        def transpose_group(g, sorted_tiles):
            i, half = divmod(g, PER_IMAGE)
            x_sb = x_tiles[i]
            grouped = gpool.tile([P, GROUP * 1024], BF16, align_bytes=64)
            for tl in range(GROUP):
                xl = half * GROUP + tl
                tbank = tps.tile([P, 512], F32, tag="tbank")
                for h in range(2):
                    for u in range(2):
                        if tl in sorted_tiles:
                            src_words = sorted_tiles[tl][:, h, u, :]
                        else:
                            src_words = words_of(x_sb)[:, h, xl, u, :]
                        slot = u * 2 + h
                        nc.tensor.transpose(
                            out=tbank[:, slot * P : (slot + 1) * P],
                            in_=src_words,
                            identity=ident_f[:],
                        )
                src = tbank[:].rearrange("p (u a y x) -> p y a x u", u=2, a=32, y=2, x=4)
                dst = (
                    grouped[:, tl * 1024 : (tl + 1) * 1024]
                    .bitcast(F32)
                    .rearrange("p (y a x u) -> p y a x u", y=2, a=32, x=4, u=2)
                )
                nc.scalar.copy(out=dst, in_=src)
            return grouped

        def new_codes():
            codes = gpool.tile([P, GROUP * 2 * P], U32, align_bytes=64)
            scales = gpool.tile([P, GROUP * 2 * P], U8, align_bytes=64)
            return codes, scales

        def quantise_tiles(grouped, codes, scales, first):
            words = slice(first * 2 * P, (first + QTILES) * 2 * P)
            nc.vector.quantize_mx(
                out=codes[:, words].bitcast(FP8X4),
                scales=scales[:, words],
                in_=grouped[:, first * 1024 : (first + QTILES) * 1024],
            )

        w_grouped = const.tile([P, 2, FOUT, 4], BF16, align_bytes=64)
        w_codes = const.tile([P, 2, FOUT], U32, align_bytes=64)
        w_scales = const.tile([P, 2, FOUT], U8, align_bytes=64)

        def prepare_w():
            for c in range(2):
                for fc in range(4):
                    if fc % 2 == 0:
                        w_bank = tps.tile([P, 4, P], F32, tag="tbank")
                    else:
                        w_bank = ops.tile([P, 4, P], F32, tag="obank")
                    for j in range(4):
                        nc.tensor.matmul(
                            out=w_bank[:, j, :],
                            lhsT=perm[:],
                            rhs=w_raw[:, c, j * FOUT + fc * P : j * FOUT + (fc + 1) * P],
                            start=True,
                            stop=True,
                        )
                    dst = w_grouped[:, c, fc * P : (fc + 1) * P, :]
                    src = w_bank[:].rearrange("p j f -> p f j")
                    if fc % 2 == 0:
                        nc.scalar.copy(out=dst, in_=src)
                    else:
                        nc.vector.tensor_copy(out=dst, in_=src)
                nc.vector.quantize_mx(
                    out=w_codes[:, c, :].bitcast(FP8X4),
                    scales=w_scales[:, c, :],
                    in_=w_grouped[:, c].rearrange("p f j -> p (f j)"),
                )

        def multiply_group(g, codes, scales, next_grouped, next_codes, next_scales):
            i, half = divmod(g, PER_IMAGE)
            o_sb = opool.tile([P, GROUP, FOUT], F32)
            dst = out[i].rearrange("(p t) f -> p t f", t=TILES)
            for tl in range(GROUP):
                xl = half * GROUP + tl
                obank = ops.tile([P, FOUT], F32, tag="obank")
                for yh in range(2):
                    cols = slice((tl * 2 + yh) * P, (tl * 2 + yh + 1) * P)
                    nc.tensor.matmul_mx(
                        out=obank[:],
                        lhsT=codes[:, cols].bitcast(FP8X4),
                        lhsT_scale=scales[:, cols],
                        rhs=w_codes[:, yh, :].bitcast(FP8X4),
                        rhs_scale=w_scales[:, yh, :],
                        start=(yh == 0),
                        stop=(yh == 1),
                    )
                nc.vector.tensor_tensor(
                    out=o_sb[:, tl, :], in0=obank[:], in1=posb[:, xl, :], op=ADD
                )
                if g >= GROUPS - TAPER:
                    nc.sync.dma_start(out=dst[:, xl : xl + 1, :], in_=o_sb[:, tl : tl + 1, :])
                if g < GROUPS - 1 and tl % QTILES == QTILES - 1:
                    quantise_tiles(next_grouped, next_codes, next_scales, tl + 1 - QTILES)
            if g < GROUPS - TAPER:
                nc.sync.dma_start(
                    out=dst[:, half * GROUP : (half + 1) * GROUP, :], in_=o_sb[:]
                )

        grouped = transpose_group(0, sort_group(0))
        codes, scales = new_codes()
        for tl in range(0, GROUP, QTILES):
            quantise_tiles(grouped, codes, scales, tl)
        prepare_posb()
        prepare_w()
        sorted_of = {1: sort_group(1)}
        next_to_sort = 2
        for g in range(GROUPS):
            next_grouped, next_codes, next_scales = None, None, None
            if g + 1 < GROUPS:
                next_grouped = transpose_group(g + 1, sorted_of[g + 1])
                next_codes, next_scales = new_codes()
                i_done, half_done = divmod(g + 1, PER_IMAGE)
                if half_done == PER_IMAGE - 1 and i_done + X_BUFS < IMAGES:
                    load_image(i_done + X_BUFS)
            ahead = SORT_AHEAD if g >= 2 else SORT_AHEAD - 1
            for k in range(next_to_sort, min(g + ahead, GROUPS - 1) + 1):
                sorted_of[k] = sort_group(k)
                next_to_sort = k + 1
            multiply_group(g, codes, scales, next_grouped, next_codes, next_scales)
            codes, scales = next_codes, next_scales
